import numpy as np
import ml_dtypes


def mxq(x, axis, fmt="e4m3"):
    dtype, down = {"e4m3": (ml_dtypes.float8_e4m3fn, 7), "e5m2": (ml_dtypes.float8_e5m2, 14)}[fmt]
    v = np.moveaxis(np.asarray(x, np.float32).astype(ml_dtypes.bfloat16).astype(np.float64), axis, -1)
    blocks = v.reshape(v.shape[:-1] + (-1, 32))
    amax = np.abs(blocks).max(-1, keepdims=True)
    byte = np.maximum(np.where(amax > 0, np.frexp(amax)[1] - 1 + 127, 0) - down, 1)
    scale = np.exp2(byte - 127.0)
    codes = (blocks / scale).astype(np.float32).astype(dtype).astype(np.float64)
    return np.moveaxis((codes * scale).reshape(v.shape), -1, axis)


WIDE = False


def mx_kscale(k):
    if not WIDE:
        return np.ones(k)
    levels = np.array([10, -10, 5, -5, 0])
    a = np.random.permutation(np.resize(levels, k // 512 * 4)).reshape(k // 512, 4)
    idx = np.arange(k)
    return np.exp2(a[idx // 512, idx % 128 // 32])


BF16 = ml_dtypes.bfloat16


def bf(x):
    return np.asarray(x, np.float32).astype(BF16)


def f64(x):
    return np.asarray(x).astype(np.float64)


T, HS, WS, WT, WH, WW, NH, HD, VID_DIM, TXT_DIM, TXT_LEN = 8, 8, 16, 8, 8, 8, 8, 128, 1536, 1536, 256
EPS = 1e-6
L_VID = T * HS * WS
N_WIN = (T // WT) * (HS // WH) * (WS // WW)
WIN_LEN = WT * WH * WW
INNER = NH * HD


def rmsnorm(x, gain):
    return x * (1.0 / np.sqrt(np.mean(x * x, axis=-1, keepdims=True) + EPS)) * gain


def window_partition(x):
    x = x.reshape(T // WT, WT, HS // WH, WH, WS // WW, WW, NH, HD)
    x = x.transpose(0, 2, 4, 1, 3, 5, 6, 7)
    return x.reshape(N_WIN, WIN_LEN, NH, HD)


def setup_inputs():
    s = mx_kscale(VID_DIM)
    return {
        "vid": bf(np.random.standard_normal((L_VID, VID_DIM)) * s),
        "Wqkv_vid": bf(np.random.standard_normal((VID_DIM, 3 * INNER)) / np.sqrt(VID_DIM) / s[:, None]),
        "bqkv_vid": bf(0.1 * np.random.standard_normal(3 * INNER)),
        "q_scale_vid": bf(1.0 + 0.1 * np.random.standard_normal(HD)),
        "k_scale_vid": bf(1.0 + 0.1 * np.random.standard_normal(HD)),
    }


def reference(vid, Wqkv_vid, bqkv_vid, q_scale_vid, k_scale_vid):
    qkv = ((mxq(f64(vid), 1, "e4m3") @ mxq(f64(Wqkv_vid), 0, "e4m3")) + f64(bqkv_vid)).reshape(L_VID, 3, NH, HD)
    q = rmsnorm(qkv[:, 0], f64(q_scale_vid))
    k = rmsnorm(qkv[:, 1], f64(k_scale_vid))
    return window_partition(q), window_partition(k), window_partition(qkv[:, 2])

@@ -1,0 +1,201 @@
+from contextlib import ExitStack
+
+import concourse.mybir as mybir
+from concourse.masks import make_identity
+
+F32 = mybir.dt.float32
+BF16 = mybir.dt.bfloat16
+I32 = mybir.dt.int32
+U32 = mybir.dt.uint32
+U8 = mybir.dt.uint8
+FP8X4 = mybir.dt.float8_e4m3fn_x4
+ACT = mybir.ActivationFunctionType
+ALU = mybir.AluOpType
+
+P = 128
+PACK = 4
+K_PASS = P * PACK
+BANK = 512
+
+TOKENS = 1024
+K = 1536
+PASSES = K // K_PASS
+PARTS = 3
+HEADS = 8
+HD = 128
+PART_COLS = HEADS * HD
+N_OUT = PARTS * PART_COLS
+HALVES = PART_COLS // BANK
+WINDOWS = 2
+WIN_W = 8
+PAIRS = TOKENS // (2 * P)
+EPS = 1e-6
+ROW_COLS = N_OUT + 2 * HD
+
+FLOPS = 2 * TOKENS * K * N_OUT
+
+
+def tile_naswinattention_pa_kernel(tc, vid, w_qkv, bias, q_gain, k_gain, out_q, out_k, out_v):
+    nc = tc.nc
+    outs = (out_q, out_k, out_v)
+
+    with ExitStack() as ctx:
+        consts = ctx.enter_context(tc.tile_pool(name="consts", bufs=1))
+        keep = ctx.enter_context(tc.tile_pool(name="keep", bufs=1))
+        stage_v = ctx.enter_context(tc.tile_pool(name="stage_v", bufs=2))
+        stage_w = ctx.enter_context(tc.tile_pool(name="stage_w", bufs=4))
+        results = ctx.enter_context(tc.tile_pool(name="results", bufs=6))
+        scratch = ctx.enter_context(tc.tile_pool(name="scratch", bufs=2))
+        stats = ctx.enter_context(tc.tile_pool(name="stats", bufs=4))
+        psum_t = ctx.enter_context(tc.psum_pool(name="psum_t", bufs=2))
+        psum_acc = ctx.enter_context(tc.psum_pool(name="psum_acc", bufs=6))
+
+        vid_pairs = vid.rearrange("(a j p) k -> a p j k", j=2, p=P)
+        vid_sb = [keep.tile([P, 2, K], BF16, name="vid_sb%d" % a) for a in range(PAIRS)]
+        w_rows = w_qkv.rearrange("(g u p e) c -> g u p e c", u=2, p=P, e=2)
+        w_raw = [
+            [keep.tile([P, PACK, PART_COLS], BF16, name="w_raw%d_%d" % (s, g)) for g in range(PASSES)]
+            for s in range(PARTS)
+        ]
+
+        def load_vid(a):
+            nc.sync.dma_start(out=vid_sb[a][:], in_=vid_pairs[a])
+
+        def load_weights(s):
+            for g in range(PASSES):
+                for u in range(2):
+                    nc.sync.dma_start(
+                        out=w_raw[s][g][:, 2 * u : 2 * u + 2, :],
+                        in_=w_rows[g, u, :, :, s * PART_COLS : (s + 1) * PART_COLS],
+                    )
+
+        load_vid(0)
+        load_weights(0)
+        for a in range(1, PAIRS):
+            load_vid(a)
+        load_weights(1)
+        load_weights(2)
+
+        ident = consts.tile([P, P], F32)
+        make_identity(nc, ident[:])
+        ones = consts.tile([P, P], BF16)
+        nc.vector.memset(ones[:], 1.0)
+        eps = consts.tile([P, 1], F32)
+        nc.vector.memset(eps[:], EPS)
+
+        rows = consts.tile([P, ROW_COLS], BF16)
+        nc.vector.memset(rows[:].bitcast(I32), 0)
+        nc.scalar.dma_start(out=rows[0:1, 0:N_OUT], in_=bias.unsqueeze(0))
+        nc.scalar.dma_start(out=rows[0:1, N_OUT : N_OUT + HD], in_=q_gain.unsqueeze(0))
+        nc.scalar.dma_start(out=rows[0:1, N_OUT + HD : ROW_COLS], in_=k_gain.unsqueeze(0))
+        spread = consts.tile([P, ROW_COLS], BF16)
+        for c0 in range(0, ROW_COLS, BANK):
+            width = min(BANK, ROW_COLS - c0)
+            summed = psum_acc.tile([P, BANK], F32, tag="acc")
+            nc.tensor.matmul(
+                out=summed[:, :width], lhsT=ones[:], rhs=rows[:, c0 : c0 + width], start=True, stop=True
+            )
+            nc.vector.tensor_copy(out=spread[:, c0 : c0 + width], in_=summed[:, :width])
+
+        v_codes = [keep.tile([P, PAIRS, WINDOWS, P], U32, name="v_codes%d" % g, align_bytes=64) for g in range(PASSES)]
+        v_scales = [keep.tile([P, PAIRS, WINDOWS, P], U8, name="v_scales%d" % g, align_bytes=64) for g in range(PASSES)]
+
+        def quantise_tokens(a):
+            words = vid_sb[a][:].bitcast(F32)
+            grouped_v = stage_v.tile([P, PASSES, WINDOWS, P * PACK], BF16, align_bytes=64)
+            grouped_words = grouped_v[:].bitcast(F32)
+            for g in range(PASSES):
+                flipped = psum_t.tile([P, 2, 2 * P], F32)
+                for u in range(2):
+                    for j in range(2):
+                        first = (2 * g + u) * P
+                        nc.tensor.transpose(
+                            flipped[:, u, j * P : (j + 1) * P], words[:, j, first : first + P], ident[:]
+                        )
+                copy = nc.vector.tensor_copy if (a * PASSES + g) % 2 == 0 else nc.scalar.copy
+                by_window = flipped[:].rearrange("p u (s n w) -> p n s w u", n=WINDOWS, w=WIN_W)
+                for n in range(WINDOWS):
+                    copy(
+                        out=grouped_words[:, g, n, :].rearrange("p (s w u) -> p s w u", w=WIN_W, u=2),
+                        in_=by_window[:, n],
+                    )
+            for g in range(PASSES):
+                nc.vector.quantize_mx(
+                    out=v_codes[g][:, a].rearrange("p n c -> p (n c)").bitcast(FP8X4),
+                    scales=v_scales[g][:, a].rearrange("p n c -> p (n c)"),
+                    in_=grouped_v[:, g].rearrange("p n c -> p (n c)"),
+                )
+
+        w_codes = [keep.tile([P, PASSES, PART_COLS], U32, name="w_codes%d" % s, align_bytes=64) for s in range(PARTS)]
+        w_scales = [keep.tile([P, PASSES, PART_COLS], U8, name="w_scales%d" % s, align_bytes=64) for s in range(PARTS)]
+
+        def quantise_weights(s, g, h):
+            cols = slice(h * BANK, (h + 1) * BANK)
+            copy = nc.vector.tensor_copy if (s == 0 and h == 0) else nc.scalar.copy
+            grouped_w = stage_w.tile([P, BANK, PACK], BF16, align_bytes=64)
+            copy(
+                out=grouped_w[:].rearrange("p (c i) t -> p c t i", i=4),
+                in_=w_raw[s][g][:, :, cols].rearrange("p t (c i) -> p c t i", i=4),
+            )
+            nc.vector.quantize_mx(
+                out=w_codes[s][:, g, cols].bitcast(FP8X4),
+                scales=w_scales[s][:, g, cols],
+                in_=grouped_w[:].rearrange("p c t -> p (c t)"),
+            )
+
+        def project(s, a, n):
+            y = results.tile([P, PART_COLS], F32)
+            for h in range(HALVES):
+                cols = slice(h * BANK, (h + 1) * BANK)
+                acc = psum_acc.tile([P, BANK], F32, tag="acc")
+                for g in range(PASSES):
+                    nc.tensor.matmul_mx(
+                        out=acc[:],
+                        lhsT=v_codes[g][:, a, n, :].bitcast(FP8X4),
+                        lhsT_scale=v_scales[g][:, a, n, :],
+                        rhs=w_codes[s][:, g, cols].bitcast(FP8X4),
+                        rhs_scale=w_scales[s][:, g, cols],
+                        start=(g == 0),
+                        stop=(g == PASSES - 1),
+                    )
+                first = s * PART_COLS + h * BANK
+                nc.vector.tensor_tensor(out=y[:, cols], in0=acc[:], in1=spread[:, first : first + BANK], op=ALU.add)
+            if s < 2:
+                gain = spread[:, N_OUT + s * HD : N_OUT + (s + 1) * HD]
+                squares = scratch.tile([P, PART_COLS], BF16)
+                sum_sq = stats.tile([P, HEADS], F32)
+                for hd in range(HEADS):
+                    head = slice(hd * HD, (hd + 1) * HD)
+                    nc.scalar.activation(
+                        out=squares[:, head], in_=y[:, head], func=ACT.Square, accum_out=sum_sq[:, hd : hd + 1]
+                    )
+                rms = stats.tile([P, HEADS], F32)
+                nc.scalar.activation(out=rms[:], in_=sum_sq[:], func=ACT.Sqrt, scale=1.0 / HD, bias=eps[:])
+                rstd = stats.tile([P, HEADS], F32)
+                nc.vector.reciprocal(out=rstd[:], in_=rms[:])
+                for hd in range(HEADS):
+                    head = slice(hd * HD, (hd + 1) * HD)
+                    nc.vector.scalar_tensor_tensor(
+                        out=y[:, head],
+                        in0=y[:, head],
+                        scalar=rstd[:, hd : hd + 1],
+                        in1=gain,
+                        op0=ALU.mult,
+                        op1=ALU.mult,
+                    )
+            nc.sync.dma_start(out=outs[s][n, a * P : (a + 1) * P].rearrange("p h d -> p (h d)"), in_=y[:])
+
+        units = [(g, h) for g in range(PASSES) for h in range(HALVES)]
+        tiles = [(a, n) for a in range(PAIRS) for n in range(WINDOWS)]
+
+        quantise_tokens(0)
+        for g, h in units:
+            quantise_weights(0, g, h)
+        for a in range(1, PAIRS):
+            quantise_tokens(a)
+        for s in range(PARTS):
+            for i, (a, n) in enumerate(tiles):
+                if s + 1 < PARTS and i < len(units):
+                    g, h = units[i]
+                    quantise_weights(s + 1, g, h)
+                project(s, a, n)

@@ -21,6 +21,7 @@ TOKENS = 1024
 K = 1536
 PASSES = K // K_PASS
 PARTS = 3
+PART_ORDER = (0, 2, 1)
 HEADS = 8
 HD = 128
 PART_COLS = HEADS * HD
@@ -50,6 +51,12 @@ def tile_naswinattention_pa_kernel(tc, vid, w_qkv, bias, q_gain, k_gain, out_q, 
         psum_t = ctx.enter_context(tc.psum_pool(name="psum_t", bufs=2))
         psum_acc = ctx.enter_context(tc.psum_pool(name="psum_acc", bufs=6))
 
+        rows = consts.tile([P, ROW_COLS], BF16)
+        nc.vector.memset(rows[:].bitcast(I32), 0)
+        nc.scalar.dma_start(out=rows[0:1, 0:N_OUT], in_=bias.unsqueeze(0))
+        nc.scalar.dma_start(out=rows[0:1, N_OUT : N_OUT + HD], in_=q_gain.unsqueeze(0))
+        nc.scalar.dma_start(out=rows[0:1, N_OUT + HD : ROW_COLS], in_=k_gain.unsqueeze(0))
+
         vid_pairs = vid.rearrange("(a j p) k -> a p j k", j=2, p=P)
         vid_sb = [keep.tile([P, 2, K], BF16, name="vid_sb%d" % a) for a in range(PAIRS)]
         w_rows = w_qkv.rearrange("(g u p e) c -> g u p e c", u=2, p=P, e=2)
@@ -70,11 +77,11 @@ def tile_naswinattention_pa_kernel(tc, vid, w_qkv, bias, q_gain, k_gain, out_q, 
                     )
 
         load_vid(0)
-        load_weights(0)
+        load_weights(PART_ORDER[0])
         for a in range(1, PAIRS):
             load_vid(a)
-        load_weights(1)
-        load_weights(2)
+        load_weights(PART_ORDER[1])
+        load_weights(PART_ORDER[2])
 
         ident = consts.tile([P, P], F32)
         make_identity(nc, ident[:])
@@ -83,19 +90,16 @@ def tile_naswinattention_pa_kernel(tc, vid, w_qkv, bias, q_gain, k_gain, out_q, 
         eps = consts.tile([P, 1], F32)
         nc.vector.memset(eps[:], EPS)
 
-        rows = consts.tile([P, ROW_COLS], BF16)
-        nc.vector.memset(rows[:].bitcast(I32), 0)
-        nc.scalar.dma_start(out=rows[0:1, 0:N_OUT], in_=bias.unsqueeze(0))
-        nc.scalar.dma_start(out=rows[0:1, N_OUT : N_OUT + HD], in_=q_gain.unsqueeze(0))
-        nc.scalar.dma_start(out=rows[0:1, N_OUT + HD : ROW_COLS], in_=k_gain.unsqueeze(0))
         spread = consts.tile([P, ROW_COLS], BF16)
-        for c0 in range(0, ROW_COLS, BANK):
-            width = min(BANK, ROW_COLS - c0)
-            summed = psum_acc.tile([P, BANK], F32, tag="acc")
-            nc.tensor.matmul(
-                out=summed[:, :width], lhsT=ones[:], rhs=rows[:, c0 : c0 + width], start=True, stop=True
-            )
-            nc.vector.tensor_copy(out=spread[:, c0 : c0 + width], in_=summed[:, :width])
+
+        def spread_constants():
+            for c0 in range(0, ROW_COLS, BANK):
+                width = min(BANK, ROW_COLS - c0)
+                summed = psum_acc.tile([P, BANK], F32, tag="acc")
+                nc.tensor.matmul(
+                    out=summed[:, :width], lhsT=ones[:], rhs=rows[:, c0 : c0 + width], start=True, stop=True
+                )
+                nc.vector.tensor_copy(out=spread[:, c0 : c0 + width], in_=summed[:, :width])
 
         v_codes = [keep.tile([P, PAIRS, WINDOWS, P], U32, name="v_codes%d" % g, align_bytes=64) for g in range(PASSES)]
         v_scales = [keep.tile([P, PAIRS, WINDOWS, P], U8, name="v_scales%d" % g, align_bytes=64) for g in range(PASSES)]
@@ -112,10 +116,9 @@ def tile_naswinattention_pa_kernel(tc, vid, w_qkv, bias, q_gain, k_gain, out_q, 
                         nc.tensor.transpose(
                             flipped[:, u, j * P : (j + 1) * P], words[:, j, first : first + P], ident[:]
                         )
-                copy = nc.vector.tensor_copy if (a * PASSES + g) % 2 == 0 else nc.scalar.copy
                 by_window = flipped[:].rearrange("p u (s n w) -> p n s w u", n=WINDOWS, w=WIN_W)
                 for n in range(WINDOWS):
-                    copy(
+                    nc.scalar.copy(
                         out=grouped_words[:, g, n, :].rearrange("p (s w u) -> p s w u", w=WIN_W, u=2),
                         in_=by_window[:, n],
                     )
@@ -131,7 +134,7 @@ def tile_naswinattention_pa_kernel(tc, vid, w_qkv, bias, q_gain, k_gain, out_q, 
 
         def quantise_weights(s, g, h):
             cols = slice(h * BANK, (h + 1) * BANK)
-            copy = nc.vector.tensor_copy if (s == 0 and h == 0) else nc.scalar.copy
+            copy = nc.vector.tensor_copy if (s == PART_ORDER[0] and h == 0) else nc.scalar.copy
             grouped_w = stage_w.tile([P, BANK, PACK], BF16, align_bytes=64)
             copy(
                 out=grouped_w[:].rearrange("p (c i) t -> p c t i", i=4),
@@ -189,13 +192,14 @@ def tile_naswinattention_pa_kernel(tc, vid, w_qkv, bias, q_gain, k_gain, out_q, 
         tiles = [(a, n) for a in range(PAIRS) for n in range(WINDOWS)]
 
         quantise_tokens(0)
+        spread_constants()
         for g, h in units:
-            quantise_weights(0, g, h)
+            quantise_weights(PART_ORDER[0], g, h)
         for a in range(1, PAIRS):
             quantise_tokens(a)
-        for s in range(PARTS):
+        for turn, s in enumerate(PART_ORDER):
             for i, (a, n) in enumerate(tiles):
-                if s + 1 < PARTS and i < len(units):
+                if turn + 1 < PARTS and i < len(units):
                     g, h = units[i]
-                    quantise_weights(s + 1, g, h)
+                    quantise_weights(PART_ORDER[turn + 1], g, h)
                 project(s, a, n)

@@ -53,9 +53,6 @@ def tile_naswinattention_pa_kernel(tc, vid, w_qkv, bias, q_gain, k_gain, out_q, 
 
         rows = consts.tile([P, ROW_COLS], BF16)
         nc.vector.memset(rows[:].bitcast(I32), 0)
-        nc.scalar.dma_start(out=rows[0:1, 0:N_OUT], in_=bias.unsqueeze(0))
-        nc.scalar.dma_start(out=rows[0:1, N_OUT : N_OUT + HD], in_=q_gain.unsqueeze(0))
-        nc.scalar.dma_start(out=rows[0:1, N_OUT + HD : ROW_COLS], in_=k_gain.unsqueeze(0))
 
         vid_pairs = vid.rearrange("(a j p) k -> a p j k", j=2, p=P)
         vid_sb = [keep.tile([P, 2, K], BF16, name="vid_sb%d" % a) for a in range(PAIRS)]
@@ -76,12 +73,16 @@ def tile_naswinattention_pa_kernel(tc, vid, w_qkv, bias, q_gain, k_gain, out_q, 
                         in_=w_rows[g, u, :, :, s * PART_COLS : (s + 1) * PART_COLS],
                     )
 
-        load_vid(0)
-        load_weights(PART_ORDER[0])
-        for a in range(1, PAIRS):
-            load_vid(a)
-        load_weights(PART_ORDER[1])
-        load_weights(PART_ORDER[2])
+        with tc.manual_schedule():
+            load_vid(0)
+            nc.sync.dma_start(out=rows[0:1, 0:N_OUT], in_=bias.unsqueeze(0))
+            nc.sync.dma_start(out=rows[0:1, N_OUT : N_OUT + HD], in_=q_gain.unsqueeze(0))
+            nc.sync.dma_start(out=rows[0:1, N_OUT + HD : ROW_COLS], in_=k_gain.unsqueeze(0))
+            load_weights(PART_ORDER[0])
+            for a in range(1, PAIRS):
+                load_vid(a)
+            load_weights(PART_ORDER[1])
+            load_weights(PART_ORDER[2])
 
         ident = consts.tile([P, P], F32)
         make_identity(nc, ident[:])
@@ -92,14 +93,12 @@ def tile_naswinattention_pa_kernel(tc, vid, w_qkv, bias, q_gain, k_gain, out_q, 
 
         spread = consts.tile([P, ROW_COLS], BF16)
 
-        def spread_constants():
-            for c0 in range(0, ROW_COLS, BANK):
-                width = min(BANK, ROW_COLS - c0)
-                summed = psum_acc.tile([P, BANK], F32, tag="acc")
-                nc.tensor.matmul(
-                    out=summed[:, :width], lhsT=ones[:], rhs=rows[:, c0 : c0 + width], start=True, stop=True
-                )
-                nc.vector.tensor_copy(out=spread[:, c0 : c0 + width], in_=summed[:, :width])
+        def spread_columns(first, width, copy):
+            summed = psum_acc.tile([P, BANK], F32, tag="acc")
+            nc.tensor.matmul(
+                out=summed[:, :width], lhsT=ones[:], rhs=rows[:, first : first + width], start=True, stop=True
+            )
+            copy(out=spread[:, first : first + width], in_=summed[:, :width])
 
         v_codes = [keep.tile([P, PAIRS, WINDOWS, P], U32, name="v_codes%d" % g, align_bytes=64) for g in range(PASSES)]
         v_scales = [keep.tile([P, PAIRS, WINDOWS, P], U8, name="v_scales%d" % g, align_bytes=64) for g in range(PASSES)]
@@ -134,7 +133,7 @@ def tile_naswinattention_pa_kernel(tc, vid, w_qkv, bias, q_gain, k_gain, out_q, 
 
         def quantise_weights(s, g, h):
             cols = slice(h * BANK, (h + 1) * BANK)
-            copy = nc.vector.tensor_copy if (s == PART_ORDER[0] and h == 0) else nc.scalar.copy
+            copy = nc.vector.tensor_copy if (s != PART_ORDER[-1] and h == 0) else nc.scalar.copy
             grouped_w = stage_w.tile([P, BANK, PACK], BF16, align_bytes=64)
             copy(
                 out=grouped_w[:].rearrange("p (c i) t -> p c t i", i=4),
@@ -172,10 +171,10 @@ def tile_naswinattention_pa_kernel(tc, vid, w_qkv, bias, q_gain, k_gain, out_q, 
                     nc.scalar.activation(
                         out=squares[:, head], in_=y[:, head], func=ACT.Square, accum_out=sum_sq[:, hd : hd + 1]
                     )
-                rms = stats.tile([P, HEADS], F32)
-                nc.scalar.activation(out=rms[:], in_=sum_sq[:], func=ACT.Sqrt, scale=1.0 / HD, bias=eps[:])
                 rstd = stats.tile([P, HEADS], F32)
-                nc.vector.reciprocal(out=rstd[:], in_=rms[:])
+                nc.scalar.activation(
+                    out=rstd[:], in_=sum_sq[:], func=ACT.Abs_reciprocal_sqrt, scale=1.0 / HD, bias=eps[:]
+                )
                 for hd in range(HEADS):
                     head = slice(hd * HD, (hd + 1) * HD)
                     nc.vector.scalar_tensor_tensor(
@@ -191,8 +190,10 @@ def tile_naswinattention_pa_kernel(tc, vid, w_qkv, bias, q_gain, k_gain, out_q, 
         units = [(g, h) for g in range(PASSES) for h in range(HALVES)]
         tiles = [(a, n) for a in range(PAIRS) for n in range(WINDOWS)]
 
+        spread_columns(N_OUT, 2 * HD, nc.vector.tensor_copy)
+        for h in range(HALVES):
+            spread_columns(PART_ORDER[0] * PART_COLS + h * BANK, BANK, nc.vector.tensor_copy)
         quantise_tokens(0)
-        spread_constants()
         for g, h in units:
             quantise_weights(PART_ORDER[0], g, h)
         for a in range(1, PAIRS):
@@ -202,4 +203,7 @@ def tile_naswinattention_pa_kernel(tc, vid, w_qkv, bias, q_gain, k_gain, out_q, 
                 if turn + 1 < PARTS and i < len(units):
                     g, h = units[i]
                     quantise_weights(PART_ORDER[turn + 1], g, h)
+                elif turn + 1 < PARTS:
+                    h = i - len(units)
+                    spread_columns(PART_ORDER[turn + 1] * PART_COLS + h * BANK, BANK, nc.scalar.copy)
                 project(s, a, n)

@@ -46,8 +46,8 @@ def tile_naswinattention_pa_kernel(tc, vid, w_qkv, bias, q_gain, k_gain, out_q, 
         stage_v = ctx.enter_context(tc.tile_pool(name="stage_v", bufs=2))
         stage_w = ctx.enter_context(tc.tile_pool(name="stage_w", bufs=4))
         results = ctx.enter_context(tc.tile_pool(name="results", bufs=6))
-        scratch = ctx.enter_context(tc.tile_pool(name="scratch", bufs=2))
-        stats = ctx.enter_context(tc.tile_pool(name="stats", bufs=4))
+        scratch = ctx.enter_context(tc.tile_pool(name="scratch", bufs=4))
+        stats = ctx.enter_context(tc.tile_pool(name="stats", bufs=8))
         psum_t = ctx.enter_context(tc.psum_pool(name="psum_t", bufs=2))
         psum_acc = ctx.enter_context(tc.psum_pool(name="psum_acc", bufs=6))
 
@@ -162,29 +162,31 @@ def tile_naswinattention_pa_kernel(tc, vid, w_qkv, bias, q_gain, k_gain, out_q, 
                     )
                 first = s * PART_COLS + h * BANK
                 nc.vector.tensor_tensor(out=y[:, cols], in0=acc[:], in1=spread[:, first : first + BANK], op=ALU.add)
-            if s < 2:
-                gain = spread[:, N_OUT + s * HD : N_OUT + (s + 1) * HD]
-                squares = scratch.tile([P, PART_COLS], BF16)
-                sum_sq = stats.tile([P, HEADS], F32)
-                for hd in range(HEADS):
-                    head = slice(hd * HD, (hd + 1) * HD)
+                if s < 2:
+                    gain = spread[:, N_OUT + s * HD : N_OUT + (s + 1) * HD]
+                    heads = [slice(c0, c0 + HD) for c0 in range(h * BANK, (h + 1) * BANK, HD)]
+                    squares = scratch.tile([P, BANK], BF16)
+                    sum_sq = stats.tile([P, len(heads)], F32)
+                    for i, head in enumerate(heads):
+                        nc.scalar.activation(
+                            out=squares[:, i * HD : (i + 1) * HD],
+                            in_=y[:, head],
+                            func=ACT.Square,
+                            accum_out=sum_sq[:, i : i + 1],
+                        )
+                    rstd = stats.tile([P, len(heads)], F32)
                     nc.scalar.activation(
-                        out=squares[:, head], in_=y[:, head], func=ACT.Square, accum_out=sum_sq[:, hd : hd + 1]
+                        out=rstd[:], in_=sum_sq[:], func=ACT.Abs_reciprocal_sqrt, scale=1.0 / HD, bias=eps[:]
                     )
-                rstd = stats.tile([P, HEADS], F32)
-                nc.scalar.activation(
-                    out=rstd[:], in_=sum_sq[:], func=ACT.Abs_reciprocal_sqrt, scale=1.0 / HD, bias=eps[:]
-                )
-                for hd in range(HEADS):
-                    head = slice(hd * HD, (hd + 1) * HD)
-                    nc.vector.scalar_tensor_tensor(
-                        out=y[:, head],
-                        in0=y[:, head],
-                        scalar=rstd[:, hd : hd + 1],
-                        in1=gain,
-                        op0=ALU.mult,
-                        op1=ALU.mult,
-                    )
+                    for i, head in enumerate(heads):
+                        nc.vector.scalar_tensor_tensor(
+                            out=y[:, head],
+                            in0=y[:, head],
+                            scalar=rstd[:, i : i + 1],
+                            in1=gain,
+                            op0=ALU.mult,
+                            op1=ALU.mult,
+                        )
             nc.sync.dma_start(out=outs[s][n, a * P : (a + 1) * P].rearrange("p h d -> p (h d)"), in_=y[:])
 
         units = [(g, h) for g in range(PASSES) for h in range(HALVES)]

@@ -56,7 +56,7 @@ def tile_naswinattention_pa_kernel(tc, vid, w_qkv, bias, q_gain, k_gain, out_q, 
 
         vid_pairs = vid.rearrange("(a j p) k -> a p j k", j=2, p=P)
         vid_sb = [keep.tile([P, 2, K], BF16, name="vid_sb%d" % a) for a in range(PAIRS)]
-        w_rows = w_qkv.rearrange("(g u p e) c -> g u p e c", u=2, p=P, e=2)
+        w_rows = w_qkv.rearrange("(g p t) c -> g p t c", p=P, t=PACK)
         w_raw = [
             [keep.tile([P, PACK, PART_COLS], BF16, name="w_raw%d_%d" % (s, g)) for g in range(PASSES)]
             for s in range(PARTS)
@@ -67,11 +67,7 @@ def tile_naswinattention_pa_kernel(tc, vid, w_qkv, bias, q_gain, k_gain, out_q, 
 
         def load_weights(s):
             for g in range(PASSES):
-                for u in range(2):
-                    nc.sync.dma_start(
-                        out=w_raw[s][g][:, 2 * u : 2 * u + 2, :],
-                        in_=w_rows[g, u, :, :, s * PART_COLS : (s + 1) * PART_COLS],
-                    )
+                nc.sync.dma_start(out=w_raw[s][g][:], in_=w_rows[g, :, :, s * PART_COLS : (s + 1) * PART_COLS])
 
         with tc.manual_schedule():
             load_vid(0)
@@ -111,9 +107,10 @@ def tile_naswinattention_pa_kernel(tc, vid, w_qkv, bias, q_gain, k_gain, out_q, 
                 flipped = psum_t.tile([P, 2, 2 * P], F32)
                 for u in range(2):
                     for j in range(2):
-                        first = (2 * g + u) * P
                         nc.tensor.transpose(
-                            flipped[:, u, j * P : (j + 1) * P], words[:, j, first : first + P], ident[:]
+                            flipped[:, u, j * P : (j + 1) * P],
+                            words[:, j, 2 * P * g + u : 2 * P * (g + 1) : 2],
+                            ident[:],
                         )
                 by_window = flipped[:].rearrange("p u (s n w) -> p n s w u", n=WINDOWS, w=WIN_W)
                 for n in range(WINDOWS):

from contextlib import ExitStack

import concourse.mybir as mybir
from concourse.masks import make_identity

F32 = mybir.dt.float32
BF16 = mybir.dt.bfloat16
I32 = mybir.dt.int32
U32 = mybir.dt.uint32
U8 = mybir.dt.uint8
FP8X4 = mybir.dt.float8_e4m3fn_x4
ACT = mybir.ActivationFunctionType
ALU = mybir.AluOpType

P = 128
PACK = 4
K_PASS = P * PACK
BANK = 512

TOKENS = 1024
K = 1536
PASSES = K // K_PASS
PARTS = 3
PART_ORDER = (0, 2, 1)
HEADS = 8
HD = 128
PART_COLS = HEADS * HD
N_OUT = PARTS * PART_COLS
HALVES = PART_COLS // BANK
WINDOWS = 2
WIN_W = 8
PAIRS = TOKENS // (2 * P)
EPS = 1e-6
ROW_COLS = N_OUT + 2 * HD

FLOPS = 2 * TOKENS * K * N_OUT


def tile_naswinattention_pa_kernel(tc, vid, w_qkv, bias, q_gain, k_gain, out_q, out_k, out_v):
    nc = tc.nc
    outs = (out_q, out_k, out_v)

    with ExitStack() as ctx:
        consts = ctx.enter_context(tc.tile_pool(name="consts", bufs=1))
        keep = ctx.enter_context(tc.tile_pool(name="keep", bufs=1))
        stage_v = ctx.enter_context(tc.tile_pool(name="stage_v", bufs=2))
        stage_w = ctx.enter_context(tc.tile_pool(name="stage_w", bufs=4))
        results = ctx.enter_context(tc.tile_pool(name="results", bufs=6))
        scratch = ctx.enter_context(tc.tile_pool(name="scratch", bufs=4))
        stats = ctx.enter_context(tc.tile_pool(name="stats", bufs=8))
        psum_t = ctx.enter_context(tc.psum_pool(name="psum_t", bufs=2))
        psum_acc = ctx.enter_context(tc.psum_pool(name="psum_acc", bufs=6))

        rows = consts.tile([P, ROW_COLS], BF16)
        nc.vector.memset(rows[:].bitcast(I32), 0)

        vid_pairs = vid.rearrange("(a j p) k -> a p j k", j=2, p=P)
        vid_sb = [keep.tile([P, 2, K], BF16, name="vid_sb%d" % a) for a in range(PAIRS)]
        w_rows = w_qkv.rearrange("(g p t) c -> g p t c", p=P, t=PACK)
        w_raw = [
            [keep.tile([P, PACK, PART_COLS], BF16, name="w_raw%d_%d" % (s, g)) for g in range(PASSES)]
            for s in range(PARTS)
        ]

        def load_vid(a):
            nc.sync.dma_start(out=vid_sb[a][:], in_=vid_pairs[a])

        def load_weights(s):
            for g in range(PASSES):
                nc.sync.dma_start(out=w_raw[s][g][:], in_=w_rows[g, :, :, s * PART_COLS : (s + 1) * PART_COLS])

        with tc.manual_schedule():
            load_vid(0)
            nc.sync.dma_start(out=rows[0:1, 0:N_OUT], in_=bias.unsqueeze(0))
            nc.sync.dma_start(out=rows[0:1, N_OUT : N_OUT + HD], in_=q_gain.unsqueeze(0))
            nc.sync.dma_start(out=rows[0:1, N_OUT + HD : ROW_COLS], in_=k_gain.unsqueeze(0))
            load_weights(PART_ORDER[0])
            for a in range(1, PAIRS):
                load_vid(a)
            load_weights(PART_ORDER[1])
            load_weights(PART_ORDER[2])

        ident = consts.tile([P, P], F32)
        make_identity(nc, ident[:])
        ones = consts.tile([P, P], BF16)
        nc.vector.memset(ones[:], 1.0)
        eps = consts.tile([P, 1], F32)
        nc.vector.memset(eps[:], EPS)

        spread = consts.tile([P, ROW_COLS], BF16)

        def spread_columns(first, width, copy):
            summed = psum_acc.tile([P, BANK], F32, tag="acc")
            nc.tensor.matmul(
                out=summed[:, :width], lhsT=ones[:], rhs=rows[:, first : first + width], start=True, stop=True
            )
            copy(out=spread[:, first : first + width], in_=summed[:, :width])

        v_codes = [keep.tile([P, PAIRS, WINDOWS, P], U32, name="v_codes%d" % g, align_bytes=64) for g in range(PASSES)]
        v_scales = [keep.tile([P, PAIRS, WINDOWS, P], U8, name="v_scales%d" % g, align_bytes=64) for g in range(PASSES)]

        def quantise_tokens(a):
            words = vid_sb[a][:].bitcast(F32)
            grouped_v = stage_v.tile([P, PASSES, WINDOWS, P * PACK], BF16, align_bytes=64)
            grouped_words = grouped_v[:].bitcast(F32)
            for g in range(PASSES):
                flipped = psum_t.tile([P, 2, 2 * P], F32)
                for u in range(2):
                    for j in range(2):
                        nc.tensor.transpose(
                            flipped[:, u, j * P : (j + 1) * P],
                            words[:, j, 2 * P * g + u : 2 * P * (g + 1) : 2],
                            ident[:],
                        )
                by_window = flipped[:].rearrange("p u (s n w) -> p n s w u", n=WINDOWS, w=WIN_W)
                for n in range(WINDOWS):
                    nc.scalar.copy(
                        out=grouped_words[:, g, n, :].rearrange("p (s w u) -> p s w u", w=WIN_W, u=2),
                        in_=by_window[:, n],
                    )
            for g in range(PASSES):
                nc.vector.quantize_mx(
                    out=v_codes[g][:, a].rearrange("p n c -> p (n c)").bitcast(FP8X4),
                    scales=v_scales[g][:, a].rearrange("p n c -> p (n c)"),
                    in_=grouped_v[:, g].rearrange("p n c -> p (n c)"),
                )

        w_codes = [keep.tile([P, PASSES, PART_COLS], U32, name="w_codes%d" % s, align_bytes=64) for s in range(PARTS)]
        w_scales = [keep.tile([P, PASSES, PART_COLS], U8, name="w_scales%d" % s, align_bytes=64) for s in range(PARTS)]

        def quantise_weights(s, g, h):
            cols = slice(h * BANK, (h + 1) * BANK)
            copy = nc.vector.tensor_copy if (s != PART_ORDER[-1] and h == 0) else nc.scalar.copy
            grouped_w = stage_w.tile([P, BANK, PACK], BF16, align_bytes=64)
            copy(
                out=grouped_w[:].rearrange("p (c i) t -> p c t i", i=4),
                in_=w_raw[s][g][:, :, cols].rearrange("p t (c i) -> p c t i", i=4),
            )
            nc.vector.quantize_mx(
                out=w_codes[s][:, g, cols].bitcast(FP8X4),
                scales=w_scales[s][:, g, cols],
                in_=grouped_w[:].rearrange("p c t -> p (c t)"),
            )

        def project(s, a, n):
            y = results.tile([P, PART_COLS], F32)
            for h in range(HALVES):
                cols = slice(h * BANK, (h + 1) * BANK)
                acc = psum_acc.tile([P, BANK], F32, tag="acc")
                for g in range(PASSES):
                    nc.tensor.matmul_mx(
                        out=acc[:],
                        lhsT=v_codes[g][:, a, n, :].bitcast(FP8X4),
                        lhsT_scale=v_scales[g][:, a, n, :],
                        rhs=w_codes[s][:, g, cols].bitcast(FP8X4),
                        rhs_scale=w_scales[s][:, g, cols],
                        start=(g == 0),
                        stop=(g == PASSES - 1),
                    )
                first = s * PART_COLS + h * BANK
                nc.vector.tensor_tensor(out=y[:, cols], in0=acc[:], in1=spread[:, first : first + BANK], op=ALU.add)
                if s < 2:
                    gain = spread[:, N_OUT + s * HD : N_OUT + (s + 1) * HD]
                    heads = [slice(c0, c0 + HD) for c0 in range(h * BANK, (h + 1) * BANK, HD)]
                    squares = scratch.tile([P, BANK], BF16)
                    sum_sq = stats.tile([P, len(heads)], F32)
                    for i, head in enumerate(heads):
                        nc.scalar.activation(
                            out=squares[:, i * HD : (i + 1) * HD],
                            in_=y[:, head],
                            func=ACT.Square,
                            accum_out=sum_sq[:, i : i + 1],
                        )
                    rstd = stats.tile([P, len(heads)], F32)
                    nc.scalar.activation(
                        out=rstd[:], in_=sum_sq[:], func=ACT.Abs_reciprocal_sqrt, scale=1.0 / HD, bias=eps[:]
                    )
                    for i, head in enumerate(heads):
                        nc.vector.scalar_tensor_tensor(
                            out=y[:, head],
                            in0=y[:, head],
                            scalar=rstd[:, i : i + 1],
                            in1=gain,
                            op0=ALU.mult,
                            op1=ALU.mult,
                        )
            nc.sync.dma_start(out=outs[s][n, a * P : (a + 1) * P].rearrange("p h d -> p (h d)"), in_=y[:])

        units = [(g, h) for g in range(PASSES) for h in range(HALVES)]
        tiles = [(a, n) for a in range(PAIRS) for n in range(WINDOWS)]

        spread_columns(N_OUT, 2 * HD, nc.vector.tensor_copy)
        for h in range(HALVES):
            spread_columns(PART_ORDER[0] * PART_COLS + h * BANK, BANK, nc.vector.tensor_copy)
        quantise_tokens(0)
        for g, h in units:
            quantise_weights(PART_ORDER[0], g, h)
        for a in range(1, PAIRS):
            quantise_tokens(a)
        for turn, s in enumerate(PART_ORDER):
            for i, (a, n) in enumerate(tiles):
                if turn + 1 < PARTS and i < len(units):
                    g, h = units[i]
                    quantise_weights(PART_ORDER[turn + 1], g, h)
                elif turn + 1 < PARTS:
                    h = i - len(units)
                    spread_columns(PART_ORDER[turn + 1] * PART_COLS + h * BANK, BANK, nc.scalar.copy)
                project(s, a, n)
